import numpy as np
import ml_dtypes


def mxq(x, axis, fmt="e4m3"):
    dtype, down = {"e4m3": (ml_dtypes.float8_e4m3fn, 7), "e5m2": (ml_dtypes.float8_e5m2, 14)}[fmt]
    v = np.moveaxis(np.asarray(x, np.float32).astype(ml_dtypes.bfloat16).astype(np.float64), axis, -1)
    blocks = v.reshape(v.shape[:-1] + (-1, 32))
    amax = np.abs(blocks).max(-1, keepdims=True)
    byte = np.maximum(np.where(amax > 0, np.frexp(amax)[1] - 1 + 127, 0) - down, 1)
    scale = np.exp2(byte - 127.0)
    codes = (blocks / scale).astype(np.float32).astype(dtype).astype(np.float64)
    return np.moveaxis((codes * scale).reshape(v.shape), -1, axis)


WIDE = False


def mx_kscale(k):
    if not WIDE:
        return np.ones(k)
    levels = np.array([10, -10, 5, -5, 0])
    a = np.random.permutation(np.resize(levels, k // 512 * 4)).reshape(k // 512, 4)
    idx = np.arange(k)
    return np.exp2(a[idx // 512, idx % 128 // 32])


BF16 = ml_dtypes.bfloat16


def bf(x):
    return np.asarray(x, np.float32).astype(BF16)


def f64(x):
    return np.asarray(x).astype(np.float64)


E2M1 = np.array([0.0, 0.5, 1.0, 1.5, 2.0, 3.0, 4.0, 6.0, -0.0, -0.5, -1.0, -1.5, -2.0, -3.0, -4.0, -6.0])


def pack_weight(w, fmt):
    k, n = w.shape
    w = f64(bf(w)).reshape(k // 32, 32, n)
    amax = np.abs(w).max(1)
    if fmt == "e4m3":
        byte = np.frexp(amax)[1] - 1 + 127 - 7
    else:
        mant, ex = np.frexp(amax / 6.0)
        byte = np.where(mant > 0.5, ex, ex - 1) + 127
    byte = np.clip(np.where(amax > 0, byte, 1), 1, 254)
    scaled = (w * np.exp2(127.0 - byte)[:, None, :]).reshape(k, n).astype(np.float32)
    by_word = np.ascontiguousarray(scaled.reshape(k // 512, 128, 4, n).transpose(0, 1, 3, 2))
    if fmt == "e4m3":
        words = by_word.astype(ml_dtypes.float8_e4m3fn).view(np.uint8)
    else:
        c = by_word.astype(ml_dtypes.float4_e2m1fn).view(np.uint8) & 0xF
        words = c[..., 0::2] | (c[..., 1::2] << 4)
    return np.ascontiguousarray(words), np.ascontiguousarray(byte.astype(np.uint8).reshape(k // 512, 16, n))


def unpack_weight(words, scales, fmt):
    g, p, n, _ = words.shape
    if fmt == "e4m3":
        vals = np.ascontiguousarray(words).view(ml_dtypes.float8_e4m3fn).astype(np.float64)
    else:
        nib = np.empty((g, p, n, 4), np.uint8)
        nib[..., 0::2] = words & 0xF
        nib[..., 1::2] = words >> 4
        vals = E2M1[nib]
    vals = vals * np.repeat(np.exp2(scales.astype(np.float64) - 127.0), 8, axis=1)[..., None]
    return vals.transpose(0, 1, 3, 2).reshape(g * 512, n)


B, S, E, H, D = 2, 512, 512, 4, 512


def setup_inputs():
    s = mx_kscale(E)
    ckv = 0.75 * D ** 0.25 / np.sqrt(E)
    cq = 3.0 / np.sqrt(E)
    x = bf(np.random.standard_normal((B, S, E)) * s)
    Wq_words, Wq_scales = pack_weight(np.random.standard_normal((E, H * D)) * cq / s[:, None], "e4m3")
    bq = bf(np.random.standard_normal(H * D) * 0.25)
    Wk_words, Wk_scales = pack_weight(np.random.standard_normal((E, H * D)) * ckv / s[:, None], "e4m3")
    bk = bf(np.random.standard_normal(H * D))
    Wv_words, Wv_scales = pack_weight(np.random.standard_normal((E, H * D)) * ckv / s[:, None], "e4m3")
    bv = bf(np.random.standard_normal(H * D))
    return {"x": x,
            "Wq_words": Wq_words, "Wq_scales": Wq_scales,
            "bq": bq,
            "Wk_words": Wk_words, "Wk_scales": Wk_scales,
            "bk": bk,
            "Wv_words": Wv_words, "Wv_scales": Wv_scales,
            "bv": bv}


def reference(x, Wq_words, Wq_scales, bq, Wk_words, Wk_scales, bk, Wv_words, Wv_scales, bv):
    xq = mxq(f64(x), 2, "e4m3")

    def proj(words, scales, bias):
        y = (xq @ unpack_weight(words, scales, "e4m3")) + f64(bias)
        return y.reshape(B, S, H, D).transpose(0, 2, 1, 3)

    q = proj(Wq_words, Wq_scales, bq)
    k = proj(Wk_words, Wk_scales, bk)
    v = proj(Wv_words, Wv_scales, bv)
    kv = k * np.swapaxes(v, -1, -2) * (1.0 / np.sqrt(D))
    e = np.exp(kv - kv.max(axis=2, keepdims=True))
    attn = e / e.sum(axis=2, keepdims=True)
    return np.sum(attn * q, axis=2)

@@ -1,0 +1,238 @@
+import math
+from contextlib import ExitStack
+
+import concourse.mybir as mybir
+from concourse.masks import make_identity
+
+F32 = mybir.dt.float32
+BF16 = mybir.dt.bfloat16
+I32 = mybir.dt.int32
+U32 = mybir.dt.uint32
+U8 = mybir.dt.uint8
+FP8X4 = mybir.dt.float8_e4m3fn_x4
+ALU = mybir.AluOpType
+ACT = mybir.ActivationFunctionType
+
+P = 128
+PACK = 4
+BATCH, SEQ, EMB, HEADS, DIM = 2, 512, 512, 4, 512
+FEATURES = HEADS * DIM
+ROW_TILES = DIM // P
+N_TILES = BATCH * HEADS * ROW_TILES
+SCORE_SCALE = 1.0 / math.sqrt(DIM)
+PLANE_ROWS = 4
+QUADRANTS = 4
+
+FLOPS = 3 * 2 * BATCH * SEQ * EMB * FEATURES
+
+
+def tile_multihead_attention_pa_kernel(
+    tc, x, Wq_words, Wq_scales, bq, Wk_words, Wk_scales, bk, Wv_words, Wv_scales, bv, out
+):
+    nc = tc.nc
+    with ExitStack() as ctx:
+        ctx.enter_context(tc.manual_schedule())
+        keep = ctx.enter_context(tc.tile_pool(name="keep", bufs=1))
+        stage = ctx.enter_context(tc.tile_pool(name="stage", bufs=2))
+        work = ctx.enter_context(tc.tile_pool(name="work", bufs=3))
+        psum = ctx.enter_context(tc.psum_pool(name="psum", bufs=8))
+
+        bv_row = keep.tile([P, FEATURES], BF16)
+        nc.vector.memset(bv_row[:], 0.0)
+        nc.scalar.dma_start(out=bv_row[0:1, :], in_=bv.rearrange("(o n) -> o n", o=1))
+        bk_rows = keep.tile([P, P], BF16)
+        nc.vector.memset(bk_rows[:], 0.0)
+        nc.scalar.dma_start(
+            out=bk_rows[0 : HEADS * ROW_TILES, :], in_=bk.rearrange("(r p) -> r p", p=P)
+        )
+        bq_rows = keep.tile([P, P], BF16)
+        nc.vector.memset(bq_rows[:], 0.0)
+        for b in range(BATCH):
+            nc.scalar.dma_start(
+                out=bq_rows[b * HEADS * ROW_TILES : (b + 1) * HEADS * ROW_TILES, :],
+                in_=bq.rearrange("(r p) -> r p", p=P),
+            )
+
+        x_sb = keep.tile([P, BATCH, SEQ // P, EMB], BF16)
+        nc.sync.dma_start(out=x_sb[:, 0], in_=x[0].rearrange("(t p) e -> p t e", p=P))
+
+        weights = {"k": (Wk_words, Wk_scales, 0), "v": (Wv_words, Wv_scales, 4), "q": (Wq_words, Wq_scales, 8)}
+        w_planes = keep.tile([P, FEATURES], U8, align_bytes=64)
+        nc.vector.memset(w_planes[:].bitcast(I32), 0)
+        w_codes = {}
+        for w in ("k", "v", "q"):
+            w_codes[w] = keep.tile([P, FEATURES], U32, name="codes_%s" % w, align_bytes=64)
+
+        def load_scales(w):
+            first_row = weights[w][2]
+            for quadrant in range(QUADRANTS):
+                rows = slice(32 * quadrant + first_row, 32 * quadrant + first_row + PLANE_ROWS)
+                nc.sync.dma_start(
+                    out=w_planes[rows, :].bitcast(I32),
+                    in_=weights[w][1][0, PLANE_ROWS * quadrant : PLANE_ROWS * (quadrant + 1), :].bitcast(I32),
+                )
+
+        def load_codes(w, h):
+            cols = slice(h * DIM, (h + 1) * DIM)
+            words = weights[w][0][0].rearrange("p n t -> p (n t)").bitcast(I32)
+            nc.sync.dma_start(out=w_codes[w][:, cols].bitcast(I32), in_=words[:, cols])
+
+        load_scales("k")
+        load_scales("v")
+        load_codes("k", 0)
+        load_codes("v", 0)
+        nc.sync.dma_start(out=x_sb[:, 1], in_=x[1].rearrange("(t p) e -> p t e", p=P))
+        load_scales("q")
+        load_codes("q", 0)
+        for h in range(1, HEADS):
+            for w in ("k", "v", "q"):
+                load_codes(w, h)
+
+        ident = keep.tile([P, P], F32)
+        make_identity(nc, ident[:])
+        ones = keep.tile([P, P], BF16)
+        nc.vector.memset(ones[:], 1.0)
+        pooled = keep.tile([P, P], F32)
+        nc.vector.memset(pooled[:], 0.0)
+        warm = keep.tile([P, 1], F32)
+        nc.vector.memset(warm[:], 0.0)
+        nc.scalar.activation(out=warm[:], in_=warm[:], func=ACT.Exp)
+
+        x_codes = keep.tile([P, BATCH * SEQ], U32, align_bytes=64)
+        x_plane = keep.tile([P, BATCH * SEQ], U8, align_bytes=64)
+
+        def quantise_batch(b):
+            grouped = stage.tile([P, SEQ * PACK], BF16, align_bytes=64)
+            grouped_words = grouped[:].bitcast(F32).rearrange("p (r u) -> p r u", u=2)
+            for half in range(2):
+                xt = psum.tile([P, 2, 2 * P], F32, tag="bank")
+                for t in range(2):
+                    words = x_sb[:, b, 2 * half + t, :].bitcast(F32)
+                    for u in range(2):
+                        nc.tensor.transpose(
+                            xt[:, u, t * P : (t + 1) * P], words[:, u : EMB // 2 : 2], ident[:]
+                        )
+                dst = grouped_words[:, half * 2 * P : (half + 1) * 2 * P, :]
+                if half == 0:
+                    nc.vector.tensor_copy(out=dst, in_=xt[:].rearrange("p u r -> p r u"))
+                else:
+                    nc.scalar.copy(out=dst, in_=xt[:].rearrange("p u r -> p r u"))
+            tokens = slice(b * SEQ, (b + 1) * SEQ)
+            nc.vector.quantize_mx(
+                out=x_codes[:, tokens].bitcast(FP8X4), scales=x_plane[:, tokens], in_=grouped[:]
+            )
+
+        quantise_batch(0)
+
+        bk_f32 = keep.tile([P, P], F32)
+        nc.vector.tensor_copy(out=bk_f32[:], in_=bk_rows[:])
+        bk_ps = psum.tile([P, P], F32, tag="bank")
+        nc.tensor.transpose(bk_ps[:], bk_f32[:], ident[:])
+        bk_cols = keep.tile([P, HEADS * ROW_TILES], F32)
+        nc.vector.tensor_scalar_mul(
+            out=bk_cols[:], in0=bk_ps[:, 0 : HEADS * ROW_TILES], scalar1=SCORE_SCALE
+        )
+        bv_all = keep.tile([P, HEADS, DIM], F32)
+        for h in range(HEADS):
+            bv_ps = psum.tile([P, DIM], F32, tag="bank")
+            nc.tensor.matmul(
+                bv_ps[:], lhsT=ones[:], rhs=bv_row[:, h * DIM : (h + 1) * DIM], start=True, stop=True
+            )
+            if h % 2 == 0:
+                nc.scalar.copy(out=bv_all[:, h, :], in_=bv_ps[:])
+            else:
+                nc.vector.tensor_copy(out=bv_all[:, h, :], in_=bv_ps[:])
+
+        quantise_batch(1)
+
+        tiles = [(b, h, r) for b in range(BATCH) for h in range(HEADS) for r in range(ROW_TILES)]
+        den = keep.tile([P, N_TILES], F32)
+        num = keep.tile([P, N_TILES], F32)
+        held = {}
+
+        def project(w, t):
+            b, h, r = tiles[t]
+            cols = slice(h * DIM + r * P, h * DIM + (r + 1) * P)
+            tokens = slice(b * SEQ, (b + 1) * SEQ)
+            acc = psum.tile([P, SEQ], F32, tag="bank", name="acc_%s" % w)
+            nc.tensor.matmul_mx(
+                out=acc[:],
+                lhsT=w_codes[w][:, cols].bitcast(FP8X4),
+                lhsT_scale=w_planes[weights[w][2] : P, cols],
+                rhs=x_codes[:, tokens].bitcast(FP8X4),
+                rhs_scale=x_plane[:, tokens],
+                start=True,
+                stop=True,
+            )
+            return acc
+
+        def factors(t):
+            b, h, r = tiles[t]
+            k_ps = project("k", t)
+            v_ps = psum.tile([P, DIM], F32, tag="bank")
+            tokens = slice(b * SEQ + r * P, b * SEQ + (r + 1) * P)
+            cols = slice(h * DIM, (h + 1) * DIM)
+            nc.tensor.matmul_mx(
+                out=v_ps[:],
+                lhsT=x_codes[:, tokens].bitcast(FP8X4),
+                lhsT_scale=x_plane[:, tokens],
+                rhs=w_codes["v"][:, cols].bitcast(FP8X4),
+                rhs_scale=w_planes[weights["v"][2] : P, cols],
+                start=True,
+                stop=True,
+            )
+            k_sb = work.tile([P, SEQ], F32)
+            c = h * ROW_TILES + r
+            nc.scalar.activation(
+                out=k_sb[:], in_=k_ps[:], func=ACT.Identity, bias=bk_cols[:, c : c + 1], scale=SCORE_SCALE
+            )
+            v_sb = work.tile([P, SEQ], F32)
+            nc.vector.tensor_tensor(out=v_sb[:], in0=v_ps[:], in1=bv_all[:, h, :], op=ALU.add)
+            held["k", t] = k_sb
+            held["v", t] = v_sb
+
+        def score(t):
+            kv = work.tile([P, SEQ], F32)
+            nc.gpsimd.tensor_tensor(out=kv[:], in0=held["k", t][:], in1=held["v", t][:], op=ALU.mult)
+            held["kv", t] = kv
+
+        def softmax(t):
+            neg_max = work.tile([P, 1], F32)
+            nc.vector.tensor_reduce(
+                out=neg_max[:], in_=held["kv", t][:], axis=mybir.AxisListType.X, op=ALU.max, negate=True
+            )
+            e = work.tile([P, SEQ], F32)
+            nc.scalar.activation(
+                out=e[:], in_=held["kv", t][:], func=ACT.Exp, bias=neg_max[:], scale=1.0,
+                accum_out=den[:, t : t + 1],
+            )
+            held["e", t] = e
+
+        def pool(t):
+            q_ps = project("q", t)
+            weighted = work.tile([P, SEQ], F32)
+            nc.vector.scalar_tensor_tensor(
+                out=weighted[:], in0=q_ps[:], scalar=1.0, in1=held["e", t][:], op0=ALU.mult, op1=ALU.mult,
+                accum_out=num[:, t : t + 1],
+            )
+
+        for step in range(N_TILES + 3):
+            if step < N_TILES:
+                factors(step)
+            if 0 <= step - 1 < N_TILES:
+                score(step - 1)
+            if 0 <= step - 2 < N_TILES:
+                softmax(step - 2)
+            if 0 <= step - 3:
+                pool(step - 3)
+
+        rden = keep.tile([P, N_TILES], F32)
+        nc.vector.reciprocal(out=rden[:], in_=den[:])
+        nc.vector.tensor_tensor(out=pooled[:, 0:N_TILES], in0=num[:], in1=rden[:], op=ALU.mult)
+        pooled_ps = psum.tile([P, P], F32, tag="bank")
+        nc.tensor.transpose(pooled_ps[:], pooled[:], ident[:])
+        out_sb = keep.tile([P, P], F32)
+        nc.vector.tensor_tensor(out=out_sb[:], in0=pooled_ps[:], in1=bq_rows[:], op=ALU.add)
+        nc.sync.dma_start(
+            out=out.rearrange("b h (r p) -> (b h r) p", p=P), in_=out_sb[0:N_TILES, :]
+        )

@@ -22,6 +22,9 @@ N_TILES = BATCH * HEADS * ROW_TILES
 SCORE_SCALE = 1.0 / math.sqrt(DIM)
 PLANE_ROWS = 4
 QUADRANTS = 4
+SCORE_LAG = 1
+SOFTMAX_LAG = 3
+POOL_LAG = 4
 
 FLOPS = 3 * 2 * BATCH * SEQ * EMB * FEATURES
 
@@ -33,32 +36,37 @@ def tile_multihead_attention_pa_kernel(
     with ExitStack() as ctx:
         ctx.enter_context(tc.manual_schedule())
         keep = ctx.enter_context(tc.tile_pool(name="keep", bufs=1))
-        stage = ctx.enter_context(tc.tile_pool(name="stage", bufs=2))
-        work = ctx.enter_context(tc.tile_pool(name="work", bufs=3))
+        work = ctx.enter_context(tc.tile_pool(name="work", bufs=4))
         psum = ctx.enter_context(tc.psum_pool(name="psum", bufs=8))
 
-        bv_row = keep.tile([P, FEATURES], BF16)
-        nc.vector.memset(bv_row[:], 0.0)
-        nc.scalar.dma_start(out=bv_row[0:1, :], in_=bv.rearrange("(o n) -> o n", o=1))
+        ident = keep.tile([P, P], F32)
+        make_identity(nc, ident[:])
+        w_planes = keep.tile([P, FEATURES], U8, align_bytes=64)
+        nc.vector.memset(w_planes[:].bitcast(I32), 0)
         bk_rows = keep.tile([P, P], BF16)
-        nc.vector.memset(bk_rows[:], 0.0)
+        nc.vector.memset(bk_rows[:].bitcast(I32), 0)
         nc.scalar.dma_start(
             out=bk_rows[0 : HEADS * ROW_TILES, :], in_=bk.rearrange("(r p) -> r p", p=P)
         )
-        bq_rows = keep.tile([P, P], BF16)
-        nc.vector.memset(bq_rows[:], 0.0)
-        for b in range(BATCH):
-            nc.scalar.dma_start(
-                out=bq_rows[b * HEADS * ROW_TILES : (b + 1) * HEADS * ROW_TILES, :],
-                in_=bq.rearrange("(r p) -> r p", p=P),
-            )
+        bv_row = keep.tile([P, FEATURES], BF16)
+        nc.vector.memset(bv_row[:].bitcast(I32), 0)
+        nc.scalar.dma_start(out=bv_row[0:1, :], in_=bv.rearrange("(o n) -> o n", o=1))
+        warm = keep.tile([P, 1], F32)
+        nc.vector.memset(warm[:], 0.0)
+        nc.scalar.activation(out=warm[:], in_=warm[:], func=ACT.Exp)
 
         x_sb = keep.tile([P, BATCH, SEQ // P, EMB], BF16)
-        nc.sync.dma_start(out=x_sb[:, 0], in_=x[0].rearrange("(t p) e -> p t e", p=P))
+
+        def load_x(b, first, count):
+            rows = x[b, first * P : (first + count) * P, :]
+            nc.sync.dma_start(
+                out=x_sb[:, b, first : first + count, :], in_=rows.rearrange("(t p) e -> p t e", p=P)
+            )
+
+        load_x(0, 0, 2)
+        load_x(0, 2, 2)
 
         weights = {"k": (Wk_words, Wk_scales, 0), "v": (Wv_words, Wv_scales, 4), "q": (Wq_words, Wq_scales, 8)}
-        w_planes = keep.tile([P, FEATURES], U8, align_bytes=64)
-        nc.vector.memset(w_planes[:].bitcast(I32), 0)
         w_codes = {}
         for w in ("k", "v", "q"):
             w_codes[w] = keep.tile([P, FEATURES], U32, name="codes_%s" % w, align_bytes=64)
@@ -81,48 +89,63 @@ def tile_multihead_attention_pa_kernel(
         load_scales("v")
         load_codes("k", 0)
         load_codes("v", 0)
-        nc.sync.dma_start(out=x_sb[:, 1], in_=x[1].rearrange("(t p) e -> p t e", p=P))
         load_scales("q")
         load_codes("q", 0)
+        load_x(1, 0, SEQ // P)
         for h in range(1, HEADS):
             for w in ("k", "v", "q"):
                 load_codes(w, h)
+        bq_rows = keep.tile([P, P], BF16)
+        nc.gpsimd.memset(bq_rows[:], 0.0)
+        for b in range(BATCH):
+            nc.sync.dma_start(
+                out=bq_rows[b * HEADS * ROW_TILES : (b + 1) * HEADS * ROW_TILES, :],
+                in_=bq.rearrange("(r p) -> r p", p=P),
+            )
 
-        ident = keep.tile([P, P], F32)
-        make_identity(nc, ident[:])
         ones = keep.tile([P, P], BF16)
         nc.vector.memset(ones[:], 1.0)
         pooled = keep.tile([P, P], F32)
-        nc.vector.memset(pooled[:], 0.0)
-        warm = keep.tile([P, 1], F32)
-        nc.vector.memset(warm[:], 0.0)
-        nc.scalar.activation(out=warm[:], in_=warm[:], func=ACT.Exp)
+        nc.gpsimd.memset(pooled[:], 0.0)
 
         x_codes = keep.tile([P, BATCH * SEQ], U32, align_bytes=64)
         x_plane = keep.tile([P, BATCH * SEQ], U8, align_bytes=64)
 
-        def quantise_batch(b):
-            grouped = stage.tile([P, SEQ * PACK], BF16, align_bytes=64)
-            grouped_words = grouped[:].bitcast(F32).rearrange("p (r u) -> p r u", u=2)
-            for half in range(2):
-                xt = psum.tile([P, 2, 2 * P], F32, tag="bank")
-                for t in range(2):
-                    words = x_sb[:, b, 2 * half + t, :].bitcast(F32)
-                    for u in range(2):
-                        nc.tensor.transpose(
-                            xt[:, u, t * P : (t + 1) * P], words[:, u : EMB // 2 : 2], ident[:]
-                        )
-                dst = grouped_words[:, half * 2 * P : (half + 1) * 2 * P, :]
-                if half == 0:
-                    nc.vector.tensor_copy(out=dst, in_=xt[:].rearrange("p u r -> p r u"))
-                else:
-                    nc.scalar.copy(out=dst, in_=xt[:].rearrange("p u r -> p r u"))
-            tokens = slice(b * SEQ, (b + 1) * SEQ)
-            nc.vector.quantize_mx(
-                out=x_codes[:, tokens].bitcast(FP8X4), scales=x_plane[:, tokens], in_=grouped[:]
+        grouped = {}
+        for b in range(BATCH):
+            grouped[b] = keep.tile([P, SEQ * PACK], BF16, name="grouped_%d" % b, align_bytes=64)
+
+        def transpose_half(b, half):
+            xt = psum.tile([P, 2, 2 * P], F32, tag="bank")
+            for t in range(2):
+                words = x_sb[:, b, 2 * half + t, :].bitcast(F32)
+                for u in range(2):
+                    nc.tensor.transpose(
+                        xt[:, u, t * P : (t + 1) * P], words[:, u : EMB // 2 : 2], ident[:]
+                    )
+            grouped_words = grouped[b][:].bitcast(F32).rearrange("p (r u) -> p r u", u=2)
+            nc.scalar.copy(
+                out=grouped_words[:, half * 2 * P : (half + 1) * 2 * P, :],
+                in_=xt[:].rearrange("p u r -> p r u"),
             )
 
-        quantise_batch(0)
+        def quantise_batch(b):
+            tokens = slice(b * SEQ, (b + 1) * SEQ)
+            nc.vector.quantize_mx(
+                out=x_codes[:, tokens].bitcast(FP8X4), scales=x_plane[:, tokens], in_=grouped[b][:]
+            )
+
+        transpose_half(0, 0)
+        transpose_half(0, 1)
+
+        bv_all = keep.tile([P, HEADS, DIM], F32)
+
+        def spread_bv(h):
+            bv_ps = psum.tile([P, DIM], F32, tag="bank")
+            nc.tensor.matmul(
+                bv_ps[:], lhsT=ones[:], rhs=bv_row[:, h * DIM : (h + 1) * DIM], start=True, stop=True
+            )
+            nc.scalar.copy(out=bv_all[:, h, :], in_=bv_ps[:])
 
         bk_f32 = keep.tile([P, P], F32)
         nc.vector.tensor_copy(out=bk_f32[:], in_=bk_rows[:])
@@ -132,18 +155,8 @@ def tile_multihead_attention_pa_kernel(
         nc.vector.tensor_scalar_mul(
             out=bk_cols[:], in0=bk_ps[:, 0 : HEADS * ROW_TILES], scalar1=SCORE_SCALE
         )
-        bv_all = keep.tile([P, HEADS, DIM], F32)
-        for h in range(HEADS):
-            bv_ps = psum.tile([P, DIM], F32, tag="bank")
-            nc.tensor.matmul(
-                bv_ps[:], lhsT=ones[:], rhs=bv_row[:, h * DIM : (h + 1) * DIM], start=True, stop=True
-            )
-            if h % 2 == 0:
-                nc.scalar.copy(out=bv_all[:, h, :], in_=bv_ps[:])
-            else:
-                nc.vector.tensor_copy(out=bv_all[:, h, :], in_=bv_ps[:])
-
-        quantise_batch(1)
+        spread_bv(0)
+        quantise_batch(0)
 
         tiles = [(b, h, r) for b in range(BATCH) for h in range(HEADS) for r in range(ROW_TILES)]
         den = keep.tile([P, N_TILES], F32)
@@ -181,13 +194,13 @@ def tile_multihead_attention_pa_kernel(
                 start=True,
                 stop=True,
             )
+            v_sb = work.tile([P, SEQ], F32)
+            nc.vector.tensor_tensor(out=v_sb[:], in0=v_ps[:], in1=bv_all[:, h, :], op=ALU.add)
             k_sb = work.tile([P, SEQ], F32)
             c = h * ROW_TILES + r
             nc.scalar.activation(
                 out=k_sb[:], in_=k_ps[:], func=ACT.Identity, bias=bk_cols[:, c : c + 1], scale=SCORE_SCALE
             )
-            v_sb = work.tile([P, SEQ], F32)
-            nc.vector.tensor_tensor(out=v_sb[:], in0=v_ps[:], in1=bv_all[:, h, :], op=ALU.add)
             held["k", t] = k_sb
             held["v", t] = v_sb
 
@@ -216,15 +229,21 @@ def tile_multihead_attention_pa_kernel(
                 accum_out=num[:, t : t + 1],
             )
 
-        for step in range(N_TILES + 3):
+        for step in range(N_TILES + POOL_LAG):
+            if 0 <= step - SCORE_LAG < N_TILES:
+                score(step - SCORE_LAG)
             if step < N_TILES:
                 factors(step)
-            if 0 <= step - 1 < N_TILES:
-                score(step - 1)
-            if 0 <= step - 2 < N_TILES:
-                softmax(step - 2)
-            if 0 <= step - 3:
-                pool(step - 3)
+            if step in (1, 3, 5):
+                spread_bv((step + 1) // 2)
+            if step in (7, 9):
+                transpose_half(1, (step - 7) // 2)
+            if step == 11:
+                quantise_batch(1)
+            if 0 <= step - SOFTMAX_LAG < N_TILES:
+                softmax(step - SOFTMAX_LAG)
+            if 0 <= step - POOL_LAG:
+                pool(step - POOL_LAG)
 
         rden = keep.tile([P, N_TILES], F32)
         nc.vector.reciprocal(out=rden[:], in_=den[:])

@@ -22,9 +22,11 @@ N_TILES = BATCH * HEADS * ROW_TILES
 SCORE_SCALE = 1.0 / math.sqrt(DIM)
 PLANE_ROWS = 4
 QUADRANTS = 4
+V_AHEAD = 6
 SCORE_LAG = 1
 SOFTMAX_LAG = 3
 POOL_LAG = 4
+HEADS_A_LOAD = 2
 
 FLOPS = 3 * 2 * BATCH * SEQ * EMB * FEATURES
 
@@ -37,24 +39,11 @@ def tile_multihead_attention_pa_kernel(
         ctx.enter_context(tc.manual_schedule())
         keep = ctx.enter_context(tc.tile_pool(name="keep", bufs=1))
         work = ctx.enter_context(tc.tile_pool(name="work", bufs=4))
+        ahead = ctx.enter_context(tc.tile_pool(name="ahead", bufs=V_AHEAD + SCORE_LAG + 2))
         psum = ctx.enter_context(tc.psum_pool(name="psum", bufs=8))
 
         ident = keep.tile([P, P], F32)
         make_identity(nc, ident[:])
-        w_planes = keep.tile([P, FEATURES], U8, align_bytes=64)
-        nc.vector.memset(w_planes[:].bitcast(I32), 0)
-        bk_rows = keep.tile([P, P], BF16)
-        nc.vector.memset(bk_rows[:].bitcast(I32), 0)
-        nc.scalar.dma_start(
-            out=bk_rows[0 : HEADS * ROW_TILES, :], in_=bk.rearrange("(r p) -> r p", p=P)
-        )
-        bv_row = keep.tile([P, FEATURES], BF16)
-        nc.vector.memset(bv_row[:].bitcast(I32), 0)
-        nc.scalar.dma_start(out=bv_row[0:1, :], in_=bv.rearrange("(o n) -> o n", o=1))
-        warm = keep.tile([P, 1], F32)
-        nc.vector.memset(warm[:], 0.0)
-        nc.scalar.activation(out=warm[:], in_=warm[:], func=ACT.Exp)
-
         x_sb = keep.tile([P, BATCH, SEQ // P, EMB], BF16)
 
         def load_x(b, first, count):
@@ -65,36 +54,50 @@ def tile_multihead_attention_pa_kernel(
 
         load_x(0, 0, 2)
         load_x(0, 2, 2)
+        bv_row = keep.tile([P, FEATURES], BF16)
+        nc.vector.memset(bv_row[:].bitcast(I32), 0)
+        nc.scalar.dma_start(out=bv_row[0:1, :], in_=bv.rearrange("(o n) -> o n", o=1))
+        w_planes = {}
+        for w in ("v", "k", "q"):
+            w_planes[w] = keep.tile([P, FEATURES], U8, name="plane_%s" % w, align_bytes=64)
+            nc.vector.memset(w_planes[w][:].bitcast(I32), 0)
+        bk_rows = keep.tile([P, P], BF16)
+        nc.vector.memset(bk_rows[:].bitcast(I32), 0)
+        warm = keep.tile([P, 1], F32)
+        nc.vector.memset(warm[:], 0.0)
+        nc.scalar.activation(out=warm[:], in_=warm[:], func=ACT.Exp)
 
-        weights = {"k": (Wk_words, Wk_scales, 0), "v": (Wv_words, Wv_scales, 4), "q": (Wq_words, Wq_scales, 8)}
+        weights = {"k": (Wk_words, Wk_scales), "v": (Wv_words, Wv_scales), "q": (Wq_words, Wq_scales)}
         w_codes = {}
         for w in ("k", "v", "q"):
             w_codes[w] = keep.tile([P, FEATURES], U32, name="codes_%s" % w, align_bytes=64)
 
         def load_scales(w):
-            first_row = weights[w][2]
             for quadrant in range(QUADRANTS):
-                rows = slice(32 * quadrant + first_row, 32 * quadrant + first_row + PLANE_ROWS)
+                rows = slice(32 * quadrant, 32 * quadrant + PLANE_ROWS)
                 nc.sync.dma_start(
-                    out=w_planes[rows, :].bitcast(I32),
+                    out=w_planes[w][rows, :].bitcast(I32),
                     in_=weights[w][1][0, PLANE_ROWS * quadrant : PLANE_ROWS * (quadrant + 1), :].bitcast(I32),
                 )
 
-        def load_codes(w, h):
-            cols = slice(h * DIM, (h + 1) * DIM)
+        def load_codes(w, part):
+            cols = slice(part * HEADS_A_LOAD * DIM, (part + 1) * HEADS_A_LOAD * DIM)
             words = weights[w][0][0].rearrange("p n t -> p (n t)").bitcast(I32)
             nc.sync.dma_start(out=w_codes[w][:, cols].bitcast(I32), in_=words[:, cols])
 
-        load_scales("k")
         load_scales("v")
-        load_codes("k", 0)
         load_codes("v", 0)
+        nc.sync.dma_start(
+            out=bk_rows[0 : HEADS * ROW_TILES, :], in_=bk.rearrange("(r p) -> r p", p=P)
+        )
+        load_codes("k", 0)
+        load_scales("k")
+        load_codes("v", 1)
         load_scales("q")
         load_codes("q", 0)
         load_x(1, 0, SEQ // P)
-        for h in range(1, HEADS):
-            for w in ("k", "v", "q"):
-                load_codes(w, h)
+        load_codes("k", 1)
+        load_codes("q", 1)
         bq_rows = keep.tile([P, P], BF16)
         nc.gpsimd.memset(bq_rows[:], 0.0)
         for b in range(BATCH):
@@ -147,16 +150,19 @@ def tile_multihead_attention_pa_kernel(
             )
             nc.scalar.copy(out=bv_all[:, h, :], in_=bv_ps[:])
 
-        bk_f32 = keep.tile([P, P], F32)
-        nc.vector.tensor_copy(out=bk_f32[:], in_=bk_rows[:])
-        bk_ps = psum.tile([P, P], F32, tag="bank")
-        nc.tensor.transpose(bk_ps[:], bk_f32[:], ident[:])
-        bk_cols = keep.tile([P, HEADS * ROW_TILES], F32)
-        nc.vector.tensor_scalar_mul(
-            out=bk_cols[:], in0=bk_ps[:, 0 : HEADS * ROW_TILES], scalar1=SCORE_SCALE
-        )
         spread_bv(0)
         quantise_batch(0)
+
+        bk_cols = keep.tile([P, HEADS * ROW_TILES], F32)
+
+        def prepare_bk():
+            bk_f32 = keep.tile([P, P], F32)
+            nc.gpsimd.tensor_copy(out=bk_f32[:], in_=bk_rows[:])
+            bk_ps = psum.tile([P, P], F32, tag="bank")
+            nc.tensor.transpose(bk_ps[:], bk_f32[:], ident[:])
+            nc.scalar.activation(
+                out=bk_cols[:], in_=bk_ps[:, 0 : HEADS * ROW_TILES], func=ACT.Copy, scale=SCORE_SCALE
+            )
 
         tiles = [(b, h, r) for b in range(BATCH) for h in range(HEADS) for r in range(ROW_TILES)]
         den = keep.tile([P, N_TILES], F32)
@@ -171,7 +177,7 @@ def tile_multihead_attention_pa_kernel(
             nc.tensor.matmul_mx(
                 out=acc[:],
                 lhsT=w_codes[w][:, cols].bitcast(FP8X4),
-                lhsT_scale=w_planes[weights[w][2] : P, cols],
+                lhsT_scale=w_planes[w][:, cols],
                 rhs=x_codes[:, tokens].bitcast(FP8X4),
                 rhs_scale=x_plane[:, tokens],
                 start=True,
@@ -179,9 +185,8 @@ def tile_multihead_attention_pa_kernel(
             )
             return acc
 
-        def factors(t):
+        def v_factor(t):
             b, h, r = tiles[t]
-            k_ps = project("k", t)
             v_ps = psum.tile([P, DIM], F32, tag="bank")
             tokens = slice(b * SEQ + r * P, b * SEQ + (r + 1) * P)
             cols = slice(h * DIM, (h + 1) * DIM)
@@ -190,19 +195,23 @@ def tile_multihead_attention_pa_kernel(
                 lhsT=x_codes[:, tokens].bitcast(FP8X4),
                 lhsT_scale=x_plane[:, tokens],
                 rhs=w_codes["v"][:, cols].bitcast(FP8X4),
-                rhs_scale=w_planes[weights["v"][2] : P, cols],
+                rhs_scale=w_planes["v"][:, cols],
                 start=True,
                 stop=True,
             )
-            v_sb = work.tile([P, SEQ], F32)
+            v_sb = ahead.tile([P, SEQ], F32)
             nc.vector.tensor_tensor(out=v_sb[:], in0=v_ps[:], in1=bv_all[:, h, :], op=ALU.add)
+            held["v", t] = v_sb
+
+        def k_factor(t):
+            b, h, r = tiles[t]
+            k_ps = project("k", t)
             k_sb = work.tile([P, SEQ], F32)
             c = h * ROW_TILES + r
             nc.scalar.activation(
                 out=k_sb[:], in_=k_ps[:], func=ACT.Identity, bias=bk_cols[:, c : c + 1], scale=SCORE_SCALE
             )
             held["k", t] = k_sb
-            held["v", t] = v_sb
 
         def score(t):
             kv = work.tile([P, SEQ], F32)
@@ -229,21 +238,26 @@ def tile_multihead_attention_pa_kernel(
                 accum_out=num[:, t : t + 1],
             )
 
-        for step in range(N_TILES + POOL_LAG):
-            if 0 <= step - SCORE_LAG < N_TILES:
-                score(step - SCORE_LAG)
+        for step in range(N_TILES + V_AHEAD + POOL_LAG):
+            u = step - V_AHEAD
+            if 0 <= u - SCORE_LAG < N_TILES:
+                score(u - SCORE_LAG)
             if step < N_TILES:
-                factors(step)
+                v_factor(step)
+            if 0 <= u < N_TILES:
+                k_factor(u)
             if step in (1, 3, 5):
                 spread_bv((step + 1) // 2)
-            if step in (7, 9):
-                transpose_half(1, (step - 7) // 2)
-            if step == 11:
+            if step == V_AHEAD - 1:
+                prepare_bk()
+            if step in (11, 12):
+                transpose_half(1, step - 11)
+            if step == 14:
                 quantise_batch(1)
-            if 0 <= step - SOFTMAX_LAG < N_TILES:
-                softmax(step - SOFTMAX_LAG)
-            if 0 <= step - POOL_LAG:
-                pool(step - POOL_LAG)
+            if 0 <= u - SOFTMAX_LAG < N_TILES:
+                softmax(u - SOFTMAX_LAG)
+            if 0 <= u - POOL_LAG < N_TILES:
+                pool(u - POOL_LAG)
 
         rden = keep.tile([P, N_TILES], F32)
         nc.vector.reciprocal(out=rden[:], in_=den[:])

@@ -22,11 +22,13 @@ N_TILES = BATCH * HEADS * ROW_TILES
 SCORE_SCALE = 1.0 / math.sqrt(DIM)
 PLANE_ROWS = 4
 QUADRANTS = 4
-V_AHEAD = 6
+V_AHEAD = 2
 SCORE_LAG = 1
 SOFTMAX_LAG = 3
 POOL_LAG = 4
-HEADS_A_LOAD = 2
+
+WARM_UP_PASSES = 3
+KEEP_UP_PASSES = 2
 
 FLOPS = 3 * 2 * BATCH * SEQ * EMB * FEATURES
 
@@ -42,6 +44,18 @@ def tile_multihead_attention_pa_kernel(
         ahead = ctx.enter_context(tc.tile_pool(name="ahead", bufs=V_AHEAD + SCORE_LAG + 2))
         psum = ctx.enter_context(tc.psum_pool(name="psum", bufs=8))
 
+        warm = keep.tile([P, 1], F32)
+        nc.vector.memset(warm[:], 0.0)
+        nc.scalar.activation(out=warm[:], in_=warm[:], func=ACT.Exp)
+        zeros = keep.tile([P, DIM], BF16)
+        nc.gpsimd.memset(zeros[:], 0.0)
+        idle_ps = psum.tile([P, DIM], F32, tag="bank")
+
+        def idle_passes(count):
+            for i in range(count):
+                nc.tensor.matmul(idle_ps[:], lhsT=zeros[:, 0:P], rhs=zeros[:], start=True, stop=True)
+
+        idle_passes(WARM_UP_PASSES)
         ident = keep.tile([P, P], F32)
         make_identity(nc, ident[:])
         x_sb = keep.tile([P, BATCH, SEQ // P, EMB], BF16)
@@ -52,20 +66,18 @@ def tile_multihead_attention_pa_kernel(
                 out=x_sb[:, b, first : first + count, :], in_=rows.rearrange("(t p) e -> p t e", p=P)
             )
 
-        load_x(0, 0, 2)
-        load_x(0, 2, 2)
-        bv_row = keep.tile([P, FEATURES], BF16)
-        nc.vector.memset(bv_row[:].bitcast(I32), 0)
-        nc.scalar.dma_start(out=bv_row[0:1, :], in_=bv.rearrange("(o n) -> o n", o=1))
+        bv_rows = keep.tile([P, DIM], BF16)
+        nc.vector.memset(bv_rows[:].bitcast(I32), 0)
         w_planes = {}
         for w in ("v", "k", "q"):
             w_planes[w] = keep.tile([P, FEATURES], U8, name="plane_%s" % w, align_bytes=64)
-            nc.vector.memset(w_planes[w][:].bitcast(I32), 0)
+        nc.vector.memset(w_planes["v"][:].bitcast(I32), 0)
+        nc.gpsimd.memset(w_planes["k"][:].bitcast(F32), 0.0)
+        ident_bf = keep.tile([P, P], BF16)
+        make_identity(nc, ident_bf[:])
         bk_rows = keep.tile([P, P], BF16)
         nc.vector.memset(bk_rows[:].bitcast(I32), 0)
-        warm = keep.tile([P, 1], F32)
-        nc.vector.memset(warm[:], 0.0)
-        nc.scalar.activation(out=warm[:], in_=warm[:], func=ACT.Exp)
+        nc.gpsimd.memset(w_planes["q"][:].bitcast(F32), 0.0)
 
         weights = {"k": (Wk_words, Wk_scales), "v": (Wv_words, Wv_scales), "q": (Wq_words, Wq_scales)}
         w_codes = {}
@@ -80,24 +92,30 @@ def tile_multihead_attention_pa_kernel(
                     in_=weights[w][1][0, PLANE_ROWS * quadrant : PLANE_ROWS * (quadrant + 1), :].bitcast(I32),
                 )
 
-        def load_codes(w, part):
-            cols = slice(part * HEADS_A_LOAD * DIM, (part + 1) * HEADS_A_LOAD * DIM)
+        def load_codes_of(w, first, count):
+            cols = slice(first * DIM, (first + count) * DIM)
             words = weights[w][0][0].rearrange("p n t -> p (n t)").bitcast(I32)
             nc.sync.dma_start(out=w_codes[w][:, cols].bitcast(I32), in_=words[:, cols])
 
+        load_x(0, 0, 1)
+        nc.sync.dma_start(out=bv_rows[0:HEADS, :], in_=bv.rearrange("(h n) -> h n", h=HEADS))
+        load_x(0, 1, SEQ // P - 1)
         load_scales("v")
-        load_codes("v", 0)
+        load_codes_of("v", 0, 1)
         nc.sync.dma_start(
             out=bk_rows[0 : HEADS * ROW_TILES, :], in_=bk.rearrange("(r p) -> r p", p=P)
         )
-        load_codes("k", 0)
         load_scales("k")
-        load_codes("v", 1)
+        load_codes_of("k", 0, 1)
+        load_codes_of("v", 1, 1)
         load_scales("q")
-        load_codes("q", 0)
+        load_codes_of("q", 0, 1)
+        load_codes_of("k", 1, 1)
+        load_codes_of("v", 2, 2)
+        load_codes_of("q", 1, 1)
+        load_codes_of("k", 2, 2)
+        load_codes_of("q", 2, 2)
         load_x(1, 0, SEQ // P)
-        load_codes("k", 1)
-        load_codes("q", 1)
         bq_rows = keep.tile([P, P], BF16)
         nc.gpsimd.memset(bq_rows[:], 0.0)
         for b in range(BATCH):
@@ -106,8 +124,6 @@ def tile_multihead_attention_pa_kernel(
                 in_=bq.rearrange("(r p) -> r p", p=P),
             )
 
-        ones = keep.tile([P, P], BF16)
-        nc.vector.memset(ones[:], 1.0)
         pooled = keep.tile([P, P], F32)
         nc.gpsimd.memset(pooled[:], 0.0)
 
@@ -138,31 +154,50 @@ def tile_multihead_attention_pa_kernel(
                 out=x_codes[:, tokens].bitcast(FP8X4), scales=x_plane[:, tokens], in_=grouped[b][:]
             )
 
-        transpose_half(0, 0)
-        transpose_half(0, 1)
+        def transpose_token_tile(b, t):
+            xt = psum.tile([P, 2, P], F32, tag="bank")
+            words = x_sb[:, b, t, :].bitcast(F32)
+            for u in range(2):
+                nc.tensor.transpose(xt[:, u, :], words[:, u : EMB // 2 : 2], ident[:])
+            grouped_words = grouped[b][:].bitcast(F32).rearrange("p (r u) -> p r u", u=2)
+            nc.scalar.copy(
+                out=grouped_words[:, t * P : (t + 1) * P, :], in_=xt[:].rearrange("p u r -> p r u")
+            )
+
+        def quantise_token_tile(b, t):
+            tokens = slice(b * SEQ + t * P, b * SEQ + (t + 1) * P)
+            nc.vector.quantize_mx(
+                out=x_codes[:, tokens].bitcast(FP8X4),
+                scales=x_plane[:, tokens],
+                in_=grouped[b][:, t * P * PACK : (t + 1) * P * PACK],
+            )
 
         bv_all = keep.tile([P, HEADS, DIM], F32)
 
         def spread_bv(h):
             bv_ps = psum.tile([P, DIM], F32, tag="bank")
             nc.tensor.matmul(
-                bv_ps[:], lhsT=ones[:], rhs=bv_row[:, h * DIM : (h + 1) * DIM], start=True, stop=True
+                bv_ps[:], lhsT=ident_bf[:, h : h + 1].to_broadcast([P, P]), rhs=bv_rows[:], start=True, stop=True
             )
             nc.scalar.copy(out=bv_all[:, h, :], in_=bv_ps[:])
 
+        transpose_token_tile(0, 0)
         spread_bv(0)
-        quantise_batch(0)
+        idle_passes(KEEP_UP_PASSES)
+        quantise_token_tile(0, 0)
+        for t in range(1, SEQ // P):
+            transpose_token_tile(0, t)
+        for t in range(1, SEQ // P):
+            quantise_token_tile(0, t)
 
         bk_cols = keep.tile([P, HEADS * ROW_TILES], F32)
 
         def prepare_bk():
-            bk_f32 = keep.tile([P, P], F32)
-            nc.gpsimd.tensor_copy(out=bk_f32[:], in_=bk_rows[:])
-            bk_ps = psum.tile([P, P], F32, tag="bank")
-            nc.tensor.transpose(bk_ps[:], bk_f32[:], ident[:])
-            nc.scalar.activation(
-                out=bk_cols[:], in_=bk_ps[:, 0 : HEADS * ROW_TILES], func=ACT.Copy, scale=SCORE_SCALE
+            bk_ps = psum.tile([P, HEADS * ROW_TILES], F32, tag="bank")
+            nc.tensor.matmul(
+                bk_ps[:], lhsT=bk_rows[:], rhs=ident_bf[:, 0 : HEADS * ROW_TILES], start=True, stop=True
             )
+            nc.scalar.activation(out=bk_cols[:], in_=bk_ps[:], func=ACT.Copy, scale=SCORE_SCALE)
 
         tiles = [(b, h, r) for b in range(BATCH) for h in range(HEADS) for r in range(ROW_TILES)]
         den = keep.tile([P, N_TILES], F32)
@@ -246,8 +281,8 @@ def tile_multihead_attention_pa_kernel(
                 v_factor(step)
             if 0 <= u < N_TILES:
                 k_factor(u)
-            if step in (1, 3, 5):
-                spread_bv((step + 1) // 2)
+            if step in (1, 5, 9):
+                spread_bv((step + 3) // 4)
             if step == V_AHEAD - 1:
                 prepare_bk()
             if step in (11, 12):

@@ -22,10 +22,13 @@ N_TILES = BATCH * HEADS * ROW_TILES
 SCORE_SCALE = 1.0 / math.sqrt(DIM)
 PLANE_ROWS = 4
 QUADRANTS = 4
-V_AHEAD = 2
-SCORE_LAG = 1
-SOFTMAX_LAG = 3
-POOL_LAG = 4
+V_AHEAD = 4
+SCORE_LAG = 2
+SOFTMAX_LAG = 7
+POOL_LAG = 9
+PAIR = 2
+N_PAIRS = N_TILES // PAIR
+RELIEVED_PAIRS = (6, 10)
 
 WARM_UP_PASSES = 3
 KEEP_UP_PASSES = 2
@@ -41,7 +44,8 @@ def tile_multihead_attention_pa_kernel(
         ctx.enter_context(tc.manual_schedule())
         keep = ctx.enter_context(tc.tile_pool(name="keep", bufs=1))
         work = ctx.enter_context(tc.tile_pool(name="work", bufs=4))
-        ahead = ctx.enter_context(tc.tile_pool(name="ahead", bufs=V_AHEAD + SCORE_LAG + 2))
+        pairs = ctx.enter_context(tc.tile_pool(name="pairs", bufs=6))
+        raw = ctx.enter_context(tc.tile_pool(name="raw", bufs=2))
         psum = ctx.enter_context(tc.psum_pool(name="psum", bufs=8))
 
         warm = keep.tile([P, 1], F32)
@@ -102,20 +106,20 @@ def tile_multihead_attention_pa_kernel(
         load_x(0, 1, SEQ // P - 1)
         load_scales("v")
         load_codes_of("v", 0, 1)
+        load_codes_of("v", 1, 1)
         nc.sync.dma_start(
             out=bk_rows[0 : HEADS * ROW_TILES, :], in_=bk.rearrange("(r p) -> r p", p=P)
         )
         load_scales("k")
         load_codes_of("k", 0, 1)
-        load_codes_of("v", 1, 1)
+        load_codes_of("v", 2, 2)
+        load_codes_of("k", 1, 1)
         load_scales("q")
         load_codes_of("q", 0, 1)
-        load_codes_of("k", 1, 1)
-        load_codes_of("v", 2, 2)
-        load_codes_of("q", 1, 1)
         load_codes_of("k", 2, 2)
-        load_codes_of("q", 2, 2)
+        load_codes_of("q", 1, 1)
         load_x(1, 0, SEQ // P)
+        load_codes_of("q", 2, 2)
         bq_rows = keep.tile([P, P], BF16)
         nc.gpsimd.memset(bq_rows[:], 0.0)
         for b in range(BATCH):
@@ -220,8 +224,12 @@ def tile_multihead_attention_pa_kernel(
             )
             return acc
 
+        def relieved(m):
+            return m in RELIEVED_PAIRS
+
         def v_factor(t):
             b, h, r = tiles[t]
+            m, half = divmod(t, PAIR)
             v_ps = psum.tile([P, DIM], F32, tag="bank")
             tokens = slice(b * SEQ + r * P, b * SEQ + (r + 1) * P)
             cols = slice(h * DIM, (h + 1) * DIM)
@@ -234,33 +242,59 @@ def tile_multihead_attention_pa_kernel(
                 start=True,
                 stop=True,
             )
-            v_sb = ahead.tile([P, SEQ], F32)
-            nc.vector.tensor_tensor(out=v_sb[:], in0=v_ps[:], in1=bv_all[:, h, :], op=ALU.add)
-            held["v", t] = v_sb
+            if half == 0:
+                v_pair = pairs.tile([P, PAIR, SEQ], F32)
+                held["v", m] = v_pair
+                if relieved(m):
+                    v_raw = raw.tile([P, PAIR, SEQ], F32)
+                    held["v_raw", m] = v_raw
+            if relieved(m):
+                nc.scalar.copy(out=held["v_raw", m][:, half, :], in_=v_ps[:])
+            else:
+                nc.vector.tensor_tensor(
+                    out=held["v", m][:, half, :], in0=v_ps[:], in1=bv_all[:, h, :], op=ALU.add
+                )
+
+        def relief_add(m):
+            h = tiles[PAIR * m][1]
+            nc.gpsimd.tensor_tensor(
+                out=held["v", m][:],
+                in0=held["v_raw", m][:],
+                in1=bv_all[:, h, :].unsqueeze(1).to_broadcast([P, PAIR, DIM]),
+                op=ALU.add,
+            )
 
         def k_factor(t):
             b, h, r = tiles[t]
+            m, half = divmod(t, PAIR)
             k_ps = project("k", t)
-            k_sb = work.tile([P, SEQ], F32)
+            if half == 0:
+                k_pair = pairs.tile([P, PAIR, SEQ], F32)
+                held["k", m] = k_pair
             c = h * ROW_TILES + r
             nc.scalar.activation(
-                out=k_sb[:], in_=k_ps[:], func=ACT.Identity, bias=bk_cols[:, c : c + 1], scale=SCORE_SCALE
+                out=held["k", m][:, half, :], in_=k_ps[:], func=ACT.Identity,
+                bias=bk_cols[:, c : c + 1], scale=SCORE_SCALE,
             )
-            held["k", t] = k_sb
 
-        def score(t):
-            kv = work.tile([P, SEQ], F32)
-            nc.gpsimd.tensor_tensor(out=kv[:], in0=held["k", t][:], in1=held["v", t][:], op=ALU.mult)
-            held["kv", t] = kv
+        def score(m):
+            kv = pairs.tile([P, PAIR, SEQ], F32)
+            nc.gpsimd.tensor_tensor(out=kv[:], in0=held["k", m][:], in1=held["v", m][:], op=ALU.mult)
+            held["kv", m] = kv
 
-        def softmax(t):
-            neg_max = work.tile([P, 1], F32)
+        def row_max(m):
+            neg_max = pairs.tile([P, PAIR], F32)
             nc.vector.tensor_reduce(
-                out=neg_max[:], in_=held["kv", t][:], axis=mybir.AxisListType.X, op=ALU.max, negate=True
+                out=neg_max[:], in_=held["kv", m][:], axis=mybir.AxisListType.X, op=ALU.max, negate=True
             )
+            held["neg_max", m] = neg_max
+
+        def exponent(t):
+            m, half = divmod(t, PAIR)
             e = work.tile([P, SEQ], F32)
             nc.scalar.activation(
-                out=e[:], in_=held["kv", t][:], func=ACT.Exp, bias=neg_max[:], scale=1.0,
+                out=e[:], in_=held["kv", m][:, half, :], func=ACT.Exp,
+                bias=held["neg_max", m][:, half : half + 1], scale=1.0,
                 accum_out=den[:, t : t + 1],
             )
             held["e", t] = e
@@ -275,8 +309,12 @@ def tile_multihead_attention_pa_kernel(
 
         for step in range(N_TILES + V_AHEAD + POOL_LAG):
             u = step - V_AHEAD
-            if 0 <= u - SCORE_LAG < N_TILES:
-                score(u - SCORE_LAG)
+            m, half = divmod(u - SCORE_LAG, PAIR)
+            if half == 0 and 0 <= m < N_PAIRS:
+                score(m)
+            m, half = divmod(step - PAIR, PAIR)
+            if half == 0 and 0 <= m < N_PAIRS and relieved(m):
+                relief_add(m)
             if step < N_TILES:
                 v_factor(step)
             if 0 <= u < N_TILES:
@@ -289,8 +327,11 @@ def tile_multihead_attention_pa_kernel(
                 transpose_half(1, step - 11)
             if step == 14:
                 quantise_batch(1)
+            m, half = divmod(u - SOFTMAX_LAG, PAIR)
+            if half == 0 and 0 <= m < N_PAIRS:
+                row_max(m)
             if 0 <= u - SOFTMAX_LAG < N_TILES:
-                softmax(u - SOFTMAX_LAG)
+                exponent(u - SOFTMAX_LAG)
             if 0 <= u - POOL_LAG < N_TILES:
                 pool(u - POOL_LAG)
 

@@ -28,7 +28,7 @@ SOFTMAX_LAG = 7
 POOL_LAG = 9
 PAIR = 2
 N_PAIRS = N_TILES // PAIR
-RELIEVED_PAIRS = (6, 10)
+RELIEVED_PAIRS = (6, 9, 12)
 
 WARM_UP_PASSES = 3
 KEEP_UP_PASSES = 2

@@ -28,7 +28,7 @@ SOFTMAX_LAG = 7
 POOL_LAG = 9
 PAIR = 2
 N_PAIRS = N_TILES // PAIR
-RELIEVED_PAIRS = (6, 9, 12)
+RELIEVED_PAIRS = (7, 10, 13)
 
 WARM_UP_PASSES = 3
 KEEP_UP_PASSES = 2

@@ -22,7 +22,7 @@ N_TILES = BATCH * HEADS * ROW_TILES
 SCORE_SCALE = 1.0 / math.sqrt(DIM)
 PLANE_ROWS = 4
 QUADRANTS = 4
-V_AHEAD = 4
+V_AHEAD = 3
 SCORE_LAG = 2
 SOFTMAX_LAG = 7
 POOL_LAG = 9
@@ -76,12 +76,12 @@ def tile_multihead_attention_pa_kernel(
         for w in ("v", "k", "q"):
             w_planes[w] = keep.tile([P, FEATURES], U8, name="plane_%s" % w, align_bytes=64)
         nc.vector.memset(w_planes["v"][:].bitcast(I32), 0)
-        nc.gpsimd.memset(w_planes["k"][:].bitcast(F32), 0.0)
         ident_bf = keep.tile([P, P], BF16)
         make_identity(nc, ident_bf[:])
+        nc.vector.memset(w_planes["k"][:].bitcast(I32), 0)
         bk_rows = keep.tile([P, P], BF16)
         nc.vector.memset(bk_rows[:].bitcast(I32), 0)
-        nc.gpsimd.memset(w_planes["q"][:].bitcast(F32), 0.0)
+        nc.vector.memset(w_planes["q"][:].bitcast(I32), 0)
 
         weights = {"k": (Wk_words, Wk_scales), "v": (Wv_words, Wv_scales), "q": (Wq_words, Wq_scales)}
         w_codes = {}
@@ -106,12 +106,12 @@ def tile_multihead_attention_pa_kernel(
         load_x(0, 1, SEQ // P - 1)
         load_scales("v")
         load_codes_of("v", 0, 1)
-        load_codes_of("v", 1, 1)
+        load_codes_of("k", 0, 1)
+        load_scales("k")
         nc.sync.dma_start(
             out=bk_rows[0 : HEADS * ROW_TILES, :], in_=bk.rearrange("(r p) -> r p", p=P)
         )
-        load_scales("k")
-        load_codes_of("k", 0, 1)
+        load_codes_of("v", 1, 1)
         load_codes_of("v", 2, 2)
         load_codes_of("k", 1, 1)
         load_scales("q")
@@ -277,17 +277,23 @@ def tile_multihead_attention_pa_kernel(
                 bias=bk_cols[:, c : c + 1], scale=SCORE_SCALE,
             )
 
-        def score(m):
-            kv = pairs.tile([P, PAIR, SEQ], F32)
-            nc.gpsimd.tensor_tensor(out=kv[:], in0=held["k", m][:], in1=held["v", m][:], op=ALU.mult)
-            held["kv", m] = kv
-
-        def row_max(m):
-            neg_max = pairs.tile([P, PAIR], F32)
-            nc.vector.tensor_reduce(
-                out=neg_max[:], in_=held["kv", m][:], axis=mybir.AxisListType.X, op=ALU.max, negate=True
+        def score(m, halves):
+            if halves.start == 0:
+                kv = pairs.tile([P, PAIR, SEQ], F32)
+                held["kv", m] = kv
+            nc.gpsimd.tensor_tensor(
+                out=held["kv", m][:, halves, :], in0=held["k", m][:, halves, :], in1=held["v", m][:, halves, :],
+                op=ALU.mult,
             )
-            held["neg_max", m] = neg_max
+
+        def row_max(m, halves):
+            if halves.start == 0:
+                neg_max = pairs.tile([P, PAIR], F32)
+                held["neg_max", m] = neg_max
+            nc.vector.tensor_reduce(
+                out=held["neg_max", m][:, halves], in_=held["kv", m][:, halves, :],
+                axis=mybir.AxisListType.X, op=ALU.max, negate=True,
+            )
 
         def exponent(t):
             m, half = divmod(t, PAIR)
@@ -310,8 +316,11 @@ def tile_multihead_attention_pa_kernel(
         for step in range(N_TILES + V_AHEAD + POOL_LAG):
             u = step - V_AHEAD
             m, half = divmod(u - SCORE_LAG, PAIR)
-            if half == 0 and 0 <= m < N_PAIRS:
-                score(m)
+            if half == 0 and 0 <= m < N_PAIRS - 1:
+                score(m, slice(0, PAIR))
+            m, half = divmod(u - 1, PAIR)
+            if m == N_PAIRS - 1:
+                score(m, slice(half, half + 1))
             m, half = divmod(step - PAIR, PAIR)
             if half == 0 and 0 <= m < N_PAIRS and relieved(m):
                 relief_add(m)
@@ -328,8 +337,10 @@ def tile_multihead_attention_pa_kernel(
             if step == 14:
                 quantise_batch(1)
             m, half = divmod(u - SOFTMAX_LAG, PAIR)
-            if half == 0 and 0 <= m < N_PAIRS:
-                row_max(m)
+            if half == 0 and 0 <= m < N_PAIRS - 1:
+                row_max(m, slice(0, PAIR))
+            if m == N_PAIRS - 1:
+                row_max(m, slice(half, half + 1))
             if 0 <= u - SOFTMAX_LAG < N_TILES:
                 exponent(u - SOFTMAX_LAG)
             if 0 <= u - POOL_LAG < N_TILES:

@@ -30,8 +30,6 @@ PAIR = 2
 N_PAIRS = N_TILES // PAIR
 RELIEVED_PAIRS = (7, 10, 13)
 
-WARM_UP_PASSES = 3
-KEEP_UP_PASSES = 2
 
 FLOPS = 3 * 2 * BATCH * SEQ * EMB * FEATURES
 
@@ -51,15 +49,6 @@ def tile_multihead_attention_pa_kernel(
         warm = keep.tile([P, 1], F32)
         nc.vector.memset(warm[:], 0.0)
         nc.scalar.activation(out=warm[:], in_=warm[:], func=ACT.Exp)
-        zeros = keep.tile([P, DIM], BF16)
-        nc.gpsimd.memset(zeros[:], 0.0)
-        idle_ps = psum.tile([P, DIM], F32, tag="bank")
-
-        def idle_passes(count):
-            for i in range(count):
-                nc.tensor.matmul(idle_ps[:], lhsT=zeros[:, 0:P], rhs=zeros[:], start=True, stop=True)
-
-        idle_passes(WARM_UP_PASSES)
         ident = keep.tile([P, P], F32)
         make_identity(nc, ident[:])
         x_sb = keep.tile([P, BATCH, SEQ // P, EMB], BF16)
@@ -187,7 +176,6 @@ def tile_multihead_attention_pa_kernel(
 
         transpose_token_tile(0, 0)
         spread_bv(0)
-        idle_passes(KEEP_UP_PASSES)
         quantise_token_tile(0, 0)
         for t in range(1, SEQ // P):
             transpose_token_tile(0, t)

@@ -165,7 +165,7 @@ def tile_multihead_attention_pa_kernel(
                 in_=grouped[b][:, t * P * PACK : (t + 1) * P * PACK],
             )
 
-        bv_all = keep.tile([P, HEADS, DIM], F32)
+        bv_all = keep.tile([P, HEADS, DIM], BF16)
 
         def spread_bv(h):
             bv_ps = psum.tile([P, DIM], F32, tag="bank")

@@ -71,6 +71,8 @@ def tile_multihead_attention_pa_kernel(
         bk_rows = keep.tile([P, P], BF16)
         nc.vector.memset(bk_rows[:].bitcast(I32), 0)
         nc.vector.memset(w_planes["q"][:].bitcast(I32), 0)
+        bq_rows = keep.tile([P, P], BF16)
+        nc.gpsimd.memset(bq_rows[:], 0.0)
 
         weights = {"k": (Wk_words, Wk_scales), "v": (Wv_words, Wv_scales), "q": (Wq_words, Wq_scales)}
         w_codes = {}
@@ -104,21 +106,14 @@ def tile_multihead_attention_pa_kernel(
         load_codes_of("v", 2, 2)
         load_codes_of("k", 1, 1)
         load_scales("q")
+        nc.sync.dma_start(
+            out=bq_rows[0 : HEADS * ROW_TILES, :], in_=bq.rearrange("(r p) -> r p", p=P)
+        )
         load_codes_of("q", 0, 1)
         load_codes_of("k", 2, 2)
         load_codes_of("q", 1, 1)
         load_x(1, 0, SEQ // P)
         load_codes_of("q", 2, 2)
-        bq_rows = keep.tile([P, P], BF16)
-        nc.gpsimd.memset(bq_rows[:], 0.0)
-        for b in range(BATCH):
-            nc.sync.dma_start(
-                out=bq_rows[b * HEADS * ROW_TILES : (b + 1) * HEADS * ROW_TILES, :],
-                in_=bq.rearrange("(r p) -> r p", p=P),
-            )
-
-        pooled = keep.tile([P, P], F32)
-        nc.gpsimd.memset(pooled[:], 0.0)
 
         x_codes = keep.tile([P, BATCH * SEQ], U32, align_bytes=64)
         x_plane = keep.tile([P, BATCH * SEQ], U8, align_bytes=64)
@@ -190,6 +185,15 @@ def tile_multihead_attention_pa_kernel(
                 bk_ps[:], lhsT=bk_rows[:], rhs=ident_bf[:, 0 : HEADS * ROW_TILES], start=True, stop=True
             )
             nc.scalar.activation(out=bk_cols[:], in_=bk_ps[:], func=ACT.Copy, scale=SCORE_SCALE)
+
+        bq_cols = keep.tile([P, HEADS * ROW_TILES], F32)
+
+        def prepare_bq():
+            bq_ps = psum.tile([P, HEADS * ROW_TILES], F32, tag="bank")
+            nc.tensor.matmul(
+                bq_ps[:], lhsT=bq_rows[:], rhs=ident_bf[:, 0 : HEADS * ROW_TILES], start=True, stop=True
+            )
+            nc.scalar.copy(out=bq_cols[:], in_=bq_ps[:])
 
         tiles = [(b, h, r) for b in range(BATCH) for h in range(HEADS) for r in range(ROW_TILES)]
         den = keep.tile([P, N_TILES], F32)
@@ -294,11 +298,13 @@ def tile_multihead_attention_pa_kernel(
             held["e", t] = e
 
         def pool(t):
+            b, h, r = tiles[t]
+            c = h * ROW_TILES + r
             q_ps = project("q", t)
             weighted = work.tile([P, SEQ], F32)
             nc.vector.scalar_tensor_tensor(
-                out=weighted[:], in0=q_ps[:], scalar=1.0, in1=held["e", t][:], op0=ALU.mult, op1=ALU.mult,
-                accum_out=num[:, t : t + 1],
+                out=weighted[:], in0=q_ps[:], scalar=bq_cols[:, c : c + 1], in1=held["e", t][:],
+                op0=ALU.add, op1=ALU.mult, accum_out=num[:, t : t + 1],
             )
 
         for step in range(N_TILES + V_AHEAD + POOL_LAG):
@@ -320,6 +326,8 @@ def tile_multihead_attention_pa_kernel(
                 spread_bv((step + 3) // 4)
             if step == V_AHEAD - 1:
                 prepare_bk()
+            if step == 10:
+                prepare_bq()
             if step in (11, 12):
                 transpose_half(1, step - 11)
             if step == 14:
@@ -336,11 +344,10 @@ def tile_multihead_attention_pa_kernel(
 
         rden = keep.tile([P, N_TILES], F32)
         nc.vector.reciprocal(out=rden[:], in_=den[:])
-        nc.vector.tensor_tensor(out=pooled[:, 0:N_TILES], in0=num[:], in1=rden[:], op=ALU.mult)
-        pooled_ps = psum.tile([P, P], F32, tag="bank")
-        nc.tensor.transpose(pooled_ps[:], pooled[:], ident[:])
-        out_sb = keep.tile([P, P], F32)
-        nc.vector.tensor_tensor(out=out_sb[:], in0=pooled_ps[:], in1=bq_rows[:], op=ALU.add)
-        nc.sync.dma_start(
-            out=out.rearrange("b h (r p) -> (b h r) p", p=P), in_=out_sb[0:N_TILES, :]
-        )
+        pooled = keep.tile([P, N_TILES], F32, align_bytes=64)
+        nc.vector.tensor_tensor(out=pooled[:], in0=num[:], in1=rden[:], op=ALU.mult)
+        turned_out = keep.tile([P, N_TILES], F32, align_bytes=64)
+        nc.vector.transpose(out=turned_out[:], in_=pooled[:])
+        rows = out.rearrange("b h (r u c) -> u (b h r) c", u=QUADRANTS, c=N_TILES)
+        for u in range(QUADRANTS):
+            nc.sync.dma_start(out=rows[u], in_=turned_out[u * N_TILES : (u + 1) * N_TILES, :])

import math
from contextlib import ExitStack

import concourse.mybir as mybir
from concourse.masks import make_identity

F32 = mybir.dt.float32
BF16 = mybir.dt.bfloat16
I32 = mybir.dt.int32
U32 = mybir.dt.uint32
U8 = mybir.dt.uint8
FP8X4 = mybir.dt.float8_e4m3fn_x4
ALU = mybir.AluOpType
ACT = mybir.ActivationFunctionType

P = 128
PACK = 4
BATCH, SEQ, EMB, HEADS, DIM = 2, 512, 512, 4, 512
FEATURES = HEADS * DIM
ROW_TILES = DIM // P
N_TILES = BATCH * HEADS * ROW_TILES
SCORE_SCALE = 1.0 / math.sqrt(DIM)
PLANE_ROWS = 4
QUADRANTS = 4
V_AHEAD = 3
SCORE_LAG = 2
SOFTMAX_LAG = 7
POOL_LAG = 9
PAIR = 2
N_PAIRS = N_TILES // PAIR
RELIEVED_PAIRS = (7, 10, 13)


FLOPS = 3 * 2 * BATCH * SEQ * EMB * FEATURES


def tile_multihead_attention_pa_kernel(
    tc, x, Wq_words, Wq_scales, bq, Wk_words, Wk_scales, bk, Wv_words, Wv_scales, bv, out
):
    nc = tc.nc
    with ExitStack() as ctx:
        ctx.enter_context(tc.manual_schedule())
        keep = ctx.enter_context(tc.tile_pool(name="keep", bufs=1))
        work = ctx.enter_context(tc.tile_pool(name="work", bufs=4))
        pairs = ctx.enter_context(tc.tile_pool(name="pairs", bufs=6))
        raw = ctx.enter_context(tc.tile_pool(name="raw", bufs=2))
        psum = ctx.enter_context(tc.psum_pool(name="psum", bufs=8))

        warm = keep.tile([P, 1], F32)
        nc.vector.memset(warm[:], 0.0)
        nc.scalar.activation(out=warm[:], in_=warm[:], func=ACT.Exp)
        ident = keep.tile([P, P], F32)
        make_identity(nc, ident[:])
        x_sb = keep.tile([P, BATCH, SEQ // P, EMB], BF16)

        def load_x(b, first, count):
            rows = x[b, first * P : (first + count) * P, :]
            nc.sync.dma_start(
                out=x_sb[:, b, first : first + count, :], in_=rows.rearrange("(t p) e -> p t e", p=P)
            )

        bv_rows = keep.tile([P, DIM], BF16)
        nc.vector.memset(bv_rows[:].bitcast(I32), 0)
        w_planes = {}
        for w in ("v", "k", "q"):
            w_planes[w] = keep.tile([P, FEATURES], U8, name="plane_%s" % w, align_bytes=64)
        nc.vector.memset(w_planes["v"][:].bitcast(I32), 0)
        ident_bf = keep.tile([P, P], BF16)
        make_identity(nc, ident_bf[:])
        nc.vector.memset(w_planes["k"][:].bitcast(I32), 0)
        bk_rows = keep.tile([P, P], BF16)
        nc.vector.memset(bk_rows[:].bitcast(I32), 0)
        nc.vector.memset(w_planes["q"][:].bitcast(I32), 0)
        bq_rows = keep.tile([P, P], BF16)
        nc.gpsimd.memset(bq_rows[:], 0.0)

        weights = {"k": (Wk_words, Wk_scales), "v": (Wv_words, Wv_scales), "q": (Wq_words, Wq_scales)}
        w_codes = {}
        for w in ("k", "v", "q"):
            w_codes[w] = keep.tile([P, FEATURES], U32, name="codes_%s" % w, align_bytes=64)

        def load_scales(w):
            for quadrant in range(QUADRANTS):
                rows = slice(32 * quadrant, 32 * quadrant + PLANE_ROWS)
                nc.sync.dma_start(
                    out=w_planes[w][rows, :].bitcast(I32),
                    in_=weights[w][1][0, PLANE_ROWS * quadrant : PLANE_ROWS * (quadrant + 1), :].bitcast(I32),
                )

        def load_codes_of(w, first, count):
            cols = slice(first * DIM, (first + count) * DIM)
            words = weights[w][0][0].rearrange("p n t -> p (n t)").bitcast(I32)
            nc.sync.dma_start(out=w_codes[w][:, cols].bitcast(I32), in_=words[:, cols])

        load_x(0, 0, 1)
        nc.sync.dma_start(out=bv_rows[0:HEADS, :], in_=bv.rearrange("(h n) -> h n", h=HEADS))
        load_x(0, 1, SEQ // P - 1)
        load_scales("v")
        load_codes_of("v", 0, 1)
        load_codes_of("k", 0, 1)
        load_scales("k")
        nc.sync.dma_start(
            out=bk_rows[0 : HEADS * ROW_TILES, :], in_=bk.rearrange("(r p) -> r p", p=P)
        )
        load_codes_of("v", 1, 1)
        load_codes_of("v", 2, 2)
        load_codes_of("k", 1, 1)
        load_scales("q")
        nc.sync.dma_start(
            out=bq_rows[0 : HEADS * ROW_TILES, :], in_=bq.rearrange("(r p) -> r p", p=P)
        )
        load_codes_of("q", 0, 1)
        load_codes_of("k", 2, 2)
        load_codes_of("q", 1, 1)
        load_x(1, 0, SEQ // P)
        load_codes_of("q", 2, 2)

        x_codes = keep.tile([P, BATCH * SEQ], U32, align_bytes=64)
        x_plane = keep.tile([P, BATCH * SEQ], U8, align_bytes=64)

        grouped = {}
        for b in range(BATCH):
            grouped[b] = keep.tile([P, SEQ * PACK], BF16, name="grouped_%d" % b, align_bytes=64)

        def transpose_half(b, half):
            xt = psum.tile([P, 2, 2 * P], F32, tag="bank")
            for t in range(2):
                words = x_sb[:, b, 2 * half + t, :].bitcast(F32)
                for u in range(2):
                    nc.tensor.transpose(
                        xt[:, u, t * P : (t + 1) * P], words[:, u : EMB // 2 : 2], ident[:]
                    )
            grouped_words = grouped[b][:].bitcast(F32).rearrange("p (r u) -> p r u", u=2)
            nc.scalar.copy(
                out=grouped_words[:, half * 2 * P : (half + 1) * 2 * P, :],
                in_=xt[:].rearrange("p u r -> p r u"),
            )

        def quantise_batch(b):
            tokens = slice(b * SEQ, (b + 1) * SEQ)
            nc.vector.quantize_mx(
                out=x_codes[:, tokens].bitcast(FP8X4), scales=x_plane[:, tokens], in_=grouped[b][:]
            )

        def transpose_token_tile(b, t):
            xt = psum.tile([P, 2, P], F32, tag="bank")
            words = x_sb[:, b, t, :].bitcast(F32)
            for u in range(2):
                nc.tensor.transpose(xt[:, u, :], words[:, u : EMB // 2 : 2], ident[:])
            grouped_words = grouped[b][:].bitcast(F32).rearrange("p (r u) -> p r u", u=2)
            nc.scalar.copy(
                out=grouped_words[:, t * P : (t + 1) * P, :], in_=xt[:].rearrange("p u r -> p r u")
            )

        def quantise_token_tile(b, t):
            tokens = slice(b * SEQ + t * P, b * SEQ + (t + 1) * P)
            nc.vector.quantize_mx(
                out=x_codes[:, tokens].bitcast(FP8X4),
                scales=x_plane[:, tokens],
                in_=grouped[b][:, t * P * PACK : (t + 1) * P * PACK],
            )

        bv_all = keep.tile([P, HEADS, DIM], BF16)

        def spread_bv(h):
            bv_ps = psum.tile([P, DIM], F32, tag="bank")
            nc.tensor.matmul(
                bv_ps[:], lhsT=ident_bf[:, h : h + 1].to_broadcast([P, P]), rhs=bv_rows[:], start=True, stop=True
            )
            nc.scalar.copy(out=bv_all[:, h, :], in_=bv_ps[:])

        transpose_token_tile(0, 0)
        spread_bv(0)
        quantise_token_tile(0, 0)
        for t in range(1, SEQ // P):
            transpose_token_tile(0, t)
        for t in range(1, SEQ // P):
            quantise_token_tile(0, t)

        bk_cols = keep.tile([P, HEADS * ROW_TILES], F32)

        def prepare_bk():
            bk_ps = psum.tile([P, HEADS * ROW_TILES], F32, tag="bank")
            nc.tensor.matmul(
                bk_ps[:], lhsT=bk_rows[:], rhs=ident_bf[:, 0 : HEADS * ROW_TILES], start=True, stop=True
            )
            nc.scalar.activation(out=bk_cols[:], in_=bk_ps[:], func=ACT.Copy, scale=SCORE_SCALE)

        bq_cols = keep.tile([P, HEADS * ROW_TILES], F32)

        def prepare_bq():
            bq_ps = psum.tile([P, HEADS * ROW_TILES], F32, tag="bank")
            nc.tensor.matmul(
                bq_ps[:], lhsT=bq_rows[:], rhs=ident_bf[:, 0 : HEADS * ROW_TILES], start=True, stop=True
            )
            nc.scalar.copy(out=bq_cols[:], in_=bq_ps[:])

        tiles = [(b, h, r) for b in range(BATCH) for h in range(HEADS) for r in range(ROW_TILES)]
        den = keep.tile([P, N_TILES], F32)
        num = keep.tile([P, N_TILES], F32)
        held = {}

        def project(w, t):
            b, h, r = tiles[t]
            cols = slice(h * DIM + r * P, h * DIM + (r + 1) * P)
            tokens = slice(b * SEQ, (b + 1) * SEQ)
            acc = psum.tile([P, SEQ], F32, tag="bank", name="acc_%s" % w)
            nc.tensor.matmul_mx(
                out=acc[:],
                lhsT=w_codes[w][:, cols].bitcast(FP8X4),
                lhsT_scale=w_planes[w][:, cols],
                rhs=x_codes[:, tokens].bitcast(FP8X4),
                rhs_scale=x_plane[:, tokens],
                start=True,
                stop=True,
            )
            return acc

        def relieved(m):
            return m in RELIEVED_PAIRS

        def v_factor(t):
            b, h, r = tiles[t]
            m, half = divmod(t, PAIR)
            v_ps = psum.tile([P, DIM], F32, tag="bank")
            tokens = slice(b * SEQ + r * P, b * SEQ + (r + 1) * P)
            cols = slice(h * DIM, (h + 1) * DIM)
            nc.tensor.matmul_mx(
                out=v_ps[:],
                lhsT=x_codes[:, tokens].bitcast(FP8X4),
                lhsT_scale=x_plane[:, tokens],
                rhs=w_codes["v"][:, cols].bitcast(FP8X4),
                rhs_scale=w_planes["v"][:, cols],
                start=True,
                stop=True,
            )
            if half == 0:
                v_pair = pairs.tile([P, PAIR, SEQ], F32)
                held["v", m] = v_pair
                if relieved(m):
                    v_raw = raw.tile([P, PAIR, SEQ], F32)
                    held["v_raw", m] = v_raw
            if relieved(m):
                nc.scalar.copy(out=held["v_raw", m][:, half, :], in_=v_ps[:])
            else:
                nc.vector.tensor_tensor(
                    out=held["v", m][:, half, :], in0=v_ps[:], in1=bv_all[:, h, :], op=ALU.add
                )

        def relief_add(m):
            h = tiles[PAIR * m][1]
            nc.gpsimd.tensor_tensor(
                out=held["v", m][:],
                in0=held["v_raw", m][:],
                in1=bv_all[:, h, :].unsqueeze(1).to_broadcast([P, PAIR, DIM]),
                op=ALU.add,
            )

        def k_factor(t):
            b, h, r = tiles[t]
            m, half = divmod(t, PAIR)
            k_ps = project("k", t)
            if half == 0:
                k_pair = pairs.tile([P, PAIR, SEQ], F32)
                held["k", m] = k_pair
            c = h * ROW_TILES + r
            nc.scalar.activation(
                out=held["k", m][:, half, :], in_=k_ps[:], func=ACT.Identity,
                bias=bk_cols[:, c : c + 1], scale=SCORE_SCALE,
            )

        def score(m, halves):
            if halves.start == 0:
                kv = pairs.tile([P, PAIR, SEQ], F32)
                held["kv", m] = kv
            nc.gpsimd.tensor_tensor(
                out=held["kv", m][:, halves, :], in0=held["k", m][:, halves, :], in1=held["v", m][:, halves, :],
                op=ALU.mult,
            )

        def row_max(m, halves):
            if halves.start == 0:
                neg_max = pairs.tile([P, PAIR], F32)
                held["neg_max", m] = neg_max
            nc.vector.tensor_reduce(
                out=held["neg_max", m][:, halves], in_=held["kv", m][:, halves, :],
                axis=mybir.AxisListType.X, op=ALU.max, negate=True,
            )

        def exponent(t):
            m, half = divmod(t, PAIR)
            e = work.tile([P, SEQ], F32)
            nc.scalar.activation(
                out=e[:], in_=held["kv", m][:, half, :], func=ACT.Exp,
                bias=held["neg_max", m][:, half : half + 1], scale=1.0,
                accum_out=den[:, t : t + 1],
            )
            held["e", t] = e

        def pool(t):
            b, h, r = tiles[t]
            c = h * ROW_TILES + r
            q_ps = project("q", t)
            weighted = work.tile([P, SEQ], F32)
            nc.vector.scalar_tensor_tensor(
                out=weighted[:], in0=q_ps[:], scalar=bq_cols[:, c : c + 1], in1=held["e", t][:],
                op0=ALU.add, op1=ALU.mult, accum_out=num[:, t : t + 1],
            )

        for step in range(N_TILES + V_AHEAD + POOL_LAG):
            u = step - V_AHEAD
            m, half = divmod(u - SCORE_LAG, PAIR)
            if half == 0 and 0 <= m < N_PAIRS - 1:
                score(m, slice(0, PAIR))
            m, half = divmod(u - 1, PAIR)
            if m == N_PAIRS - 1:
                score(m, slice(half, half + 1))
            m, half = divmod(step - PAIR, PAIR)
            if half == 0 and 0 <= m < N_PAIRS and relieved(m):
                relief_add(m)
            if step < N_TILES:
                v_factor(step)
            if 0 <= u < N_TILES:
                k_factor(u)
            if step in (1, 5, 9):
                spread_bv((step + 3) // 4)
            if step == V_AHEAD - 1:
                prepare_bk()
            if step == 10:
                prepare_bq()
            if step in (11, 12):
                transpose_half(1, step - 11)
            if step == 14:
                quantise_batch(1)
            m, half = divmod(u - SOFTMAX_LAG, PAIR)
            if half == 0 and 0 <= m < N_PAIRS - 1:
                row_max(m, slice(0, PAIR))
            if m == N_PAIRS - 1:
                row_max(m, slice(half, half + 1))
            if 0 <= u - SOFTMAX_LAG < N_TILES:
                exponent(u - SOFTMAX_LAG)
            if 0 <= u - POOL_LAG < N_TILES:
                pool(u - POOL_LAG)

        rden = keep.tile([P, N_TILES], F32)
        nc.vector.reciprocal(out=rden[:], in_=den[:])
        pooled = keep.tile([P, N_TILES], F32, align_bytes=64)
        nc.vector.tensor_tensor(out=pooled[:], in0=num[:], in1=rden[:], op=ALU.mult)
        turned_out = keep.tile([P, N_TILES], F32, align_bytes=64)
        nc.vector.transpose(out=turned_out[:], in_=pooled[:])
        rows = out.rearrange("b h (r u c) -> u (b h r) c", u=QUADRANTS, c=N_TILES)
        for u in range(QUADRANTS):
            nc.sync.dma_start(out=rows[u], in_=turned_out[u * N_TILES : (u + 1) * N_TILES, :])
